import numpy as np
import ml_dtypes


def mxq(x, axis, fmt="e4m3"):
    dtype, down = {"e4m3": (ml_dtypes.float8_e4m3fn, 7), "e5m2": (ml_dtypes.float8_e5m2, 14)}[fmt]
    v = np.moveaxis(np.asarray(x, np.float32).astype(ml_dtypes.bfloat16).astype(np.float64), axis, -1)
    blocks = v.reshape(v.shape[:-1] + (-1, 32))
    amax = np.abs(blocks).max(-1, keepdims=True)
    byte = np.maximum(np.where(amax > 0, np.frexp(amax)[1] - 1 + 127, 0) - down, 1)
    scale = np.exp2(byte - 127.0)
    codes = (blocks / scale).astype(np.float32).astype(dtype).astype(np.float64)
    return np.moveaxis((codes * scale).reshape(v.shape), -1, axis)


WIDE = False


def mx_kscale(k):
    if not WIDE:
        return np.ones(k)
    levels = np.array([10, -10, 5, -5, 0])
    a = np.random.permutation(np.resize(levels, k // 512 * 4)).reshape(k // 512, 4)
    idx = np.arange(k)
    return np.exp2(a[idx // 512, idx % 128 // 32])


BF16 = ml_dtypes.bfloat16


def bf(x):
    return np.asarray(x, np.float32).astype(BF16)


def f64(x):
    return np.asarray(x).astype(np.float64)


B, S, D, H, HD, FF = 2, 256, 1024, 8, 128, 4096
ROT = HD // 4
EPS = 1e-5
ROPE_BASE = 10000.0


def layernorm(x, g, b):
    mu = x.mean(-1, keepdims=True)
    var = np.square(x - mu).mean(-1, keepdims=True)
    return (x - mu) / np.sqrt(var + EPS) * g + b


def rope_cos_sin():
    inv_freq = 1.0 / ROPE_BASE ** (np.arange(0, ROT, 2) / ROT)
    freqs = np.outer(np.arange(S), inv_freq)
    emb = np.concatenate([freqs, freqs], -1)
    return np.cos(emb), np.sin(emb)


def apply_rope(x, cos, sin):
    half = x.shape[-1] // 2
    x1, x2 = x[..., :half], x[..., half:]
    rot = np.concatenate([-x2, x1], -1)
    return x * cos[None, None, :, :] + rot * sin[None, None, :, :]


def setup_inputs():
    s = mx_kscale(D)
    return {"hidden_states": bf(np.random.standard_normal((B, S, D))),
            "ln1_g": bf((1.0 + 0.1 * np.random.standard_normal(D)) * s),
            "ln1_b": bf(0.1 * np.random.standard_normal(D) * s),
            "W_qkv": bf(np.random.standard_normal((D, 3 * H * HD)) / np.sqrt(D) / s[:, None]),
            "b_qkv": bf(0.3 * np.random.standard_normal(3 * H * HD))}


def reference(hidden_states, ln1_g, ln1_b, W_qkv, b_qkv):
    x = layernorm(f64(hidden_states), f64(ln1_g), f64(ln1_b))
    qkv = ((mxq(x, 2, "e4m3") @ mxq(f64(W_qkv), 0, "e4m3")) + f64(b_qkv)).reshape(B, S, H, 3 * HD)
    q = np.transpose(qkv[..., :HD], (0, 2, 1, 3))
    k = np.transpose(qkv[..., HD:2 * HD], (0, 2, 1, 3))
    v = np.transpose(qkv[..., 2 * HD:], (0, 2, 1, 3))
    cos, sin = rope_cos_sin()
    q = np.concatenate([apply_rope(q[..., :ROT], cos, sin), q[..., ROT:]], -1)
    k = np.concatenate([apply_rope(k[..., :ROT], cos, sin), k[..., ROT:]], -1)
    return q, k, v

@@ -1,0 +1,338 @@
+import math
+from contextlib import ExitStack
+
+import concourse.mybir as mybir
+from concourse.masks import make_identity
+
+F32 = mybir.dt.float32
+BF16 = mybir.dt.bfloat16
+I32 = mybir.dt.int32
+U32 = mybir.dt.uint32
+U8 = mybir.dt.uint8
+FP8X4 = mybir.dt.float8_e4m3fn_x4
+ALU = mybir.AluOpType
+ACT = mybir.ActivationFunctionType
+
+P = 128
+B, S, D, H, HD = 2, 256, 1024, 8, 128
+ROT = HD // 4
+HALF = ROT // 2
+EPS = 1e-5
+ROPE_BASE = 10000.0
+PACK = 4
+PASSES = D // (P * PACK)
+K_CHUNKS = D // P
+PARITY = S // P
+CHUNK_HEADS = 2
+CHUNKS = H // CHUNK_HEADS
+HEAD_COLS = 3 * HD
+CHUNK_COLS = CHUNK_HEADS * HEAD_COLS
+QK_COLS = CHUNK_HEADS * 2 * HD
+V_COLS = CHUNK_HEADS * HD
+BN_FMAX = 512
+BN_STATS_DIM = 6
+ROUND_MAGIC = 1.5 * 2.0**23
+
+FLOPS = 2 * B * S * D * 3 * H * HD
+
+
+def regroup(copy, dst, src):
+    copy(
+        out=dst.rearrange("p (c i) t -> p c t i", i=4),
+        in_=src.rearrange("p t (c i) -> p c t i", i=4),
+    )
+
+
+def tile_customgptneoxlayer_pa_kernel(
+    tc, hidden_states, ln1_g, ln1_b, W_qkv, b_qkv, out_0, out_1, out_2
+):
+    nc = tc.nc
+    outs = (out_0, out_1, out_2)
+    with ExitStack() as stack:
+        consts = stack.enter_context(tc.tile_pool(name="consts", bufs=1))
+        xpool = stack.enter_context(tc.tile_pool(name="xpool", bufs=1))
+        wpool = stack.enter_context(tc.tile_pool(name="wpool", bufs=1))
+        stage = stack.enter_context(tc.tile_pool(name="stage", bufs=3))
+        respool = stack.enter_context(tc.tile_pool(name="respool", bufs=4))
+        psum = stack.enter_context(tc.psum_pool(name="psum", bufs=8))
+
+        x_sb = []
+        for b in range(B):
+            x_b = xpool.tile([P, PARITY, D], BF16, name="x_sb%d" % b)
+            nc.sync.dma_start(
+                out=x_b[:], in_=hidden_states[b].rearrange("(p e) d -> p e d", e=PARITY)
+            )
+            x_sb.append(x_b)
+        gb_rows = consts.tile([P, P], BF16)
+        nc.vector.memset(gb_rows[:], 0.0)
+        nc.sync.dma_start(
+            out=gb_rows[0:K_CHUNKS, :], in_=ln1_g.rearrange("(a p) -> a p", p=P)
+        )
+        nc.sync.dma_start(
+            out=gb_rows[K_CHUNKS : 2 * K_CHUNKS, :],
+            in_=ln1_b.rearrange("(a p) -> a p", p=P),
+        )
+        w_rows = W_qkv.rearrange("(a p) n -> p a n", p=P)
+        bias_bc = consts.tile([P, H, 3, HD], BF16)
+        wraw = []
+        for c in range(CHUNKS):
+            w_c = wpool.tile([P, K_CHUNKS, CHUNK_COLS], BF16, name="wraw%d" % c)
+            nc.sync.dma_start(
+                out=w_c[:], in_=w_rows[:, :, CHUNK_COLS * c : CHUNK_COLS * (c + 1)]
+            )
+            wraw.append(w_c)
+            if c == 0:
+                nc.sync.dma_start(
+                    out=bias_bc[:].rearrange("p h w d -> p (h w d)"),
+                    in_=b_qkv.partition_broadcast(P),
+                )
+
+        ident_f32 = consts.tile([P, P], F32)
+        make_identity(nc, ident_f32[:])
+        ident_bf16 = consts.tile([P, P], BF16)
+        nc.vector.tensor_copy(out=ident_bf16[:], in_=ident_f32[:])
+        neg_half = consts.tile([P, PARITY], F32)
+        nc.vector.memset(neg_half[:], -0.5)
+
+        pos_i = consts.tile([P, PARITY], I32)
+        nc.gpsimd.iota(pos_i[:], pattern=[[1, PARITY]], base=0, channel_multiplier=PARITY)
+        pos = consts.tile([P, PARITY], F32)
+        nc.vector.tensor_copy(out=pos[:], in_=pos_i[:])
+        turns = consts.tile([P, 2, PARITY, HALF], F32)
+        for j in range(HALF):
+            nc.vector.tensor_scalar(
+                out=turns[:, 1, :, j],
+                in0=pos[:],
+                scalar1=ROPE_BASE ** (-j / HALF) / (2.0 * math.pi),
+                scalar2=None,
+                op0=ALU.mult,
+            )
+        nc.vector.tensor_scalar(
+            out=turns[:, 0], in0=turns[:, 1], scalar1=0.25, scalar2=None, op0=ALU.add
+        )
+        whole = consts.tile([P, 2, PARITY, HALF], F32)
+        nc.vector.tensor_scalar(
+            out=whole[:],
+            in0=turns[:],
+            scalar1=ROUND_MAGIC,
+            scalar2=ROUND_MAGIC,
+            op0=ALU.add,
+            op1=ALU.subtract,
+        )
+        frac = consts.tile([P, 2, PARITY, HALF], F32)
+        nc.vector.tensor_tensor(out=frac[:], in0=turns[:], in1=whole[:], op=ALU.subtract)
+        cos_tab = consts.tile([P, PARITY, 2, HALF], F32)
+        sin_tab = consts.tile([P, PARITY, 2, HALF], F32)
+        nc.scalar.activation(
+            out=cos_tab[:],
+            in_=frac[:, 0].unsqueeze(2).to_broadcast([P, PARITY, 2, HALF]),
+            func=ACT.Sin,
+            scale=2.0 * math.pi,
+        )
+        nc.scalar.activation(
+            out=sin_tab[:, :, 0, :], in_=frac[:, 1], func=ACT.Sin, scale=-2.0 * math.pi
+        )
+        nc.scalar.activation(
+            out=sin_tab[:, :, 1, :], in_=frac[:, 1], func=ACT.Sin, scale=2.0 * math.pi
+        )
+
+        gb_t = psum.tile([P, P], BF16, tag="bank")
+        nc.tensor.transpose(gb_t[:], gb_rows[:], ident_bf16[:])
+        gb_cols = consts.tile([P, 2 * K_CHUNKS], F32)
+        nc.vector.tensor_copy(out=gb_cols[:], in_=gb_t[:, 0 : 2 * K_CHUNKS])
+
+        xb = xpool.tile([P, K_CHUNKS, B * S], BF16)
+        xcodes = xpool.tile([P, PASSES, B * S], U32, align_bytes=64)
+        xscales = xpool.tile([P, PASSES, B * S], U8, align_bytes=64)
+        for b in range(B):
+            stats = xpool.tile(
+                [P, PARITY, D // BN_FMAX, BN_STATS_DIM], F32, name="stats%d" % b
+            )
+            mean_var = xpool.tile([P, PARITY, 2], F32, name="mean_var%d" % b)
+            for e in range(PARITY):
+                for f in range(D // BN_FMAX):
+                    nc.vector.bn_stats(
+                        out=stats[:, e, f, :],
+                        in_=x_sb[b][:, e, BN_FMAX * f : BN_FMAX * (f + 1)],
+                    )
+                nc.vector.bn_aggr(
+                    out=mean_var[:, e, :], in_=stats[:, e].rearrange("p f s -> p (f s)")
+                )
+            neg_mean = xpool.tile([P, PARITY], F32, name="neg_mean%d" % b)
+            nc.vector.tensor_scalar(
+                out=neg_mean[:], in0=mean_var[:, :, 0], scalar1=-1.0, scalar2=None, op0=ALU.mult
+            )
+            var_eps = xpool.tile([P, PARITY], F32, name="var_eps%d" % b)
+            nc.vector.tensor_scalar(
+                out=var_eps[:], in0=mean_var[:, :, 1], scalar1=EPS, scalar2=None, op0=ALU.add
+            )
+            rstd = xpool.tile([P, PARITY], F32, name="rstd%d" % b)
+            nc.gpsimd.tensor_tensor(out=rstd[:], in0=var_eps[:], in1=neg_half[:], op=ALU.pow)
+            xn = xpool.tile([P, PARITY, D], F32, name="xn%d" % b)
+            for e in range(PARITY):
+                nc.gpsimd.tensor_scalar(
+                    out=xn[:, e, :],
+                    in0=x_sb[b][:, e, :],
+                    scalar1=neg_mean[:, e : e + 1],
+                    scalar2=rstd[:, e : e + 1],
+                    op0=ALU.add,
+                    op1=ALU.mult,
+                )
+            cols = slice(S * b, S * (b + 1))
+            for i in range(K_CHUNKS // 2):
+                xt = psum.tile([P, 2, S], F32, tag="bank")
+                for ai in range(2):
+                    a = 2 * i + ai
+                    for e in range(PARITY):
+                        nc.tensor.transpose(
+                            xt[:, ai, P * e : P * (e + 1)],
+                            xn[:, e, P * a : P * (a + 1)],
+                            ident_f32[:],
+                        )
+                for ai in range(2):
+                    a = 2 * i + ai
+                    gain = gb_cols[:, a : a + 1]
+                    shift = gb_cols[:, K_CHUNKS + a : K_CHUNKS + a + 1]
+                    if i % 2 == 0:
+                        nc.scalar.activation(
+                            out=xb[:, a, cols],
+                            in_=xt[:, ai, :],
+                            func=ACT.Identity,
+                            scale=gain,
+                            bias=shift,
+                        )
+                    else:
+                        nc.vector.tensor_scalar(
+                            out=xb[:, a, cols],
+                            in0=xt[:, ai, :],
+                            scalar1=gain,
+                            scalar2=shift,
+                            op0=ALU.mult,
+                            op1=ALU.add,
+                        )
+            for g in range(PASSES):
+                xg = xpool.tile([P, S, PACK], BF16, name="xg%d_%d" % (b, g), align_bytes=64)
+                regroup(nc.vector.tensor_copy, xg[:], xb[:, PACK * g : PACK * (g + 1), cols])
+                nc.vector.quantize_mx(
+                    out=xcodes[:, g, cols].bitcast(FP8X4),
+                    scales=xscales[:, g, cols],
+                    in_=xg[:].rearrange("p c t -> p (c t)"),
+                )
+
+        wcodes = []
+        wscales = []
+
+        def prepare_weights(c):
+            codes = wpool.tile([P, PASSES, CHUNK_COLS], U32, name="wcodes%d" % c, align_bytes=64)
+            scales = wpool.tile([P, PASSES, CHUNK_COLS], U8, name="wscales%d" % c, align_bytes=64)
+            for g in range(PASSES):
+                rows = wraw[c][:, PACK * g : PACK * (g + 1), :]
+                wg_qk = stage.tile([P, QK_COLS, PACK], BF16, align_bytes=64)
+                wg_v = stage.tile([P, V_COLS, PACK], BF16, align_bytes=64)
+                for h in range(CHUNK_HEADS):
+                    head = HEAD_COLS * h
+                    regroup(
+                        nc.scalar.copy,
+                        wg_qk[:, 2 * HD * h : 2 * HD * (h + 1), :],
+                        rows[:, :, head : head + 2 * HD],
+                    )
+                    regroup(
+                        nc.vector.tensor_copy,
+                        wg_v[:, HD * h : HD * (h + 1), :],
+                        rows[:, :, head + 2 * HD : head + 3 * HD],
+                    )
+                nc.vector.quantize_mx(
+                    out=codes[:, g, 0:QK_COLS].bitcast(FP8X4),
+                    scales=scales[:, g, 0:QK_COLS],
+                    in_=wg_qk[:].rearrange("p c t -> p (c t)"),
+                )
+                nc.vector.quantize_mx(
+                    out=codes[:, g, QK_COLS:CHUNK_COLS].bitcast(FP8X4),
+                    scales=scales[:, g, QK_COLS:CHUNK_COLS],
+                    in_=wg_v[:].rearrange("p c t -> p (c t)"),
+                )
+            wcodes.append(codes)
+            wscales.append(scales)
+
+        def mx_group(acc, b, e, c, w_cols):
+            tokens = slice(S * b + P * e, S * b + P * (e + 1))
+            for g in range(PASSES):
+                nc.tensor.matmul_mx(
+                    out=acc,
+                    lhsT=xcodes[:, g, tokens].bitcast(FP8X4),
+                    lhsT_scale=xscales[:, g, tokens],
+                    rhs=wcodes[c][:, g, w_cols].bitcast(FP8X4),
+                    rhs_scale=wscales[c][:, g, w_cols],
+                    start=(g == 0),
+                    stop=(g == PASSES - 1),
+                )
+
+        def project(c, b):
+            heads = slice(CHUNK_HEADS * c, CHUNK_HEADS * (c + 1))
+            res = respool.tile([P, 3, CHUNK_HEADS, PARITY, HD], F32)
+            for e in range(PARITY):
+                acc_qk = psum.tile([P, CHUNK_HEADS, 2, HD], F32, tag="bank")
+                mx_group(acc_qk[:].rearrange("p h w d -> p (h w d)"), b, e, c, slice(0, QK_COLS))
+                nc.vector.tensor_tensor(
+                    out=res[:, 0:2, :, e, :].rearrange("p w h d -> p h w d"),
+                    in0=acc_qk[:],
+                    in1=bias_bc[:, heads, 0:2, :],
+                    op=ALU.add,
+                )
+            acc_v = psum.tile([P, PARITY, CHUNK_HEADS, HD], F32, tag="bank")
+            for e in range(PARITY):
+                mx_group(
+                    acc_v[:, e].rearrange("p h d -> p (h d)"), b, e, c, slice(QK_COLS, CHUNK_COLS)
+                )
+            nc.vector.tensor_tensor(
+                out=res[:, 2].rearrange("p h e d -> p e h d"),
+                in0=acc_v[:],
+                in1=bias_bc[:, heads, 2, :].unsqueeze(1).to_broadcast([P, PARITY, CHUNK_HEADS, HD]),
+                op=ALU.add,
+            )
+            nc.sync.dma_start(
+                out=outs[2][b, heads].rearrange("h (p e) d -> p h (e d)", e=PARITY),
+                in_=res[:, 2].rearrange("p h e d -> p h (e d)"),
+            )
+            blocks = 2 * CHUNK_HEADS
+            u = res[:, 0:2, :, :, 0:ROT].rearrange("p w h e j -> p (w h) e j")
+            cos_b = (
+                cos_tab[:]
+                .rearrange("p e s j -> p e (s j)")
+                .unsqueeze(1)
+                .to_broadcast([P, blocks, PARITY, ROT])
+            )
+            sin_b = (
+                sin_tab[:]
+                .rearrange("p e s j -> p e (s j)")
+                .unsqueeze(1)
+                .to_broadcast([P, blocks, PARITY, ROT])
+            )
+            straight = respool.tile([P, blocks, PARITY, ROT], F32)
+            crossed = respool.tile([P, blocks, PARITY, ROT], F32)
+            nc.gpsimd.tensor_tensor(out=straight[:], in0=u, in1=cos_b, op=ALU.mult)
+            nc.gpsimd.tensor_tensor(
+                out=crossed[:, :, :, 0:HALF],
+                in0=u[:, :, :, HALF:ROT],
+                in1=sin_b[:, :, :, 0:HALF],
+                op=ALU.mult,
+            )
+            nc.gpsimd.tensor_tensor(
+                out=crossed[:, :, :, HALF:ROT],
+                in0=u[:, :, :, 0:HALF],
+                in1=sin_b[:, :, :, HALF:ROT],
+                op=ALU.mult,
+            )
+            nc.gpsimd.tensor_tensor(out=u, in0=straight[:], in1=crossed[:], op=ALU.add)
+            for w in range(2):
+                nc.sync.dma_start(
+                    out=outs[w][b, heads].rearrange("h (p e) d -> p h (e d)", e=PARITY),
+                    in_=res[:, w].rearrange("p h e d -> p h (e d)"),
+                )
+
+        prepare_weights(0)
+        for c in range(CHUNKS):
+            if c + 1 < CHUNKS:
+                prepare_weights(c + 1)
+            for b in range(B):
+                project(c, b)

@@ -25,10 +25,10 @@ K_CHUNKS = D // P
 PARITY = S // P
 CHUNK_HEADS = 2
 CHUNKS = H // CHUNK_HEADS
-HEAD_COLS = 3 * HD
-CHUNK_COLS = CHUNK_HEADS * HEAD_COLS
-QK_COLS = CHUNK_HEADS * 2 * HD
-V_COLS = CHUNK_HEADS * HD
+CHUNK_BLOCKS = 3 * CHUNK_HEADS
+CHUNK_COLS = CHUNK_BLOCKS * HD
+WIDE_BLOCKS = 4
+WIDE_COLS = WIDE_BLOCKS * HD
 BN_FMAX = 512
 BN_STATS_DIM = 6
 ROUND_MAGIC = 1.5 * 2.0**23
@@ -48,54 +48,80 @@ def tile_customgptneoxlayer_pa_kernel(
 ):
     nc = tc.nc
     outs = (out_0, out_1, out_2)
+    wide = slice(0, WIDE_COLS)
+    narrow = slice(WIDE_COLS, CHUNK_COLS)
     with ExitStack() as stack:
         consts = stack.enter_context(tc.tile_pool(name="consts", bufs=1))
         xpool = stack.enter_context(tc.tile_pool(name="xpool", bufs=1))
         wpool = stack.enter_context(tc.tile_pool(name="wpool", bufs=1))
         stage = stack.enter_context(tc.tile_pool(name="stage", bufs=3))
-        respool = stack.enter_context(tc.tile_pool(name="respool", bufs=4))
+        respool = stack.enter_context(tc.tile_pool(name="respool", bufs=1))
+        ropepool = stack.enter_context(tc.tile_pool(name="ropepool", bufs=2))
         psum = stack.enter_context(tc.psum_pool(name="psum", bufs=8))
+        stack.enter_context(tc.manual_schedule())
 
-        x_sb = []
-        for b in range(B):
-            x_b = xpool.tile([P, PARITY, D], BF16, name="x_sb%d" % b)
+        param_rows = consts.tile([P, P], BF16)
+        x_sb = [xpool.tile([P, PARITY, D], BF16, name="x_sb%d" % b) for b in range(B)]
+        xn = [xpool.tile([P, PARITY, D], F32, name="xn%d" % b) for b in range(B)]
+        wraw = [
+            [wpool.tile([P, PACK, CHUNK_COLS], BF16, name="wraw%d_%d" % (c, g)) for g in range(PASSES)]
+            for c in range(CHUNKS)
+        ]
+        bias_bc = [consts.tile([P, CHUNK_BLOCKS, HD], BF16, name="bias_bc%d" % c) for c in range(CHUNKS)]
+        wcodes = [
+            wpool.tile([P, PASSES, CHUNK_COLS], U32, name="wcodes%d" % c, align_bytes=64)
+            for c in range(CHUNKS)
+        ]
+        wscales = [
+            wpool.tile([P, PASSES, CHUNK_COLS], U8, name="wscales%d" % c, align_bytes=64)
+            for c in range(CHUNKS)
+        ]
+        xb = xpool.tile([P, K_CHUNKS, B * S], BF16)
+        xcodes = xpool.tile([P, PASSES, B * S], U32, align_bytes=64)
+        xscales = xpool.tile([P, PASSES, B * S], U8, align_bytes=64)
+        res = [
+            respool.tile([P, B, CHUNK_HEADS, 3, PARITY, HD], F32, name="res%d" % c)
+            for c in range(CHUNKS)
+        ]
+
+        nc.vector.memset(param_rows[:], 0.0)
+        nc.sync.dma_start(out=param_rows[0:K_CHUNKS, :], in_=ln1_g.rearrange("(a p) -> a p", p=P))
+        nc.sync.dma_start(
+            out=param_rows[K_CHUNKS : 2 * K_CHUNKS, :], in_=ln1_b.rearrange("(a p) -> a p", p=P)
+        )
+
+        def load_x(b):
             nc.sync.dma_start(
-                out=x_b[:], in_=hidden_states[b].rearrange("(p e) d -> p e d", e=PARITY)
+                out=x_sb[b][:], in_=hidden_states[b].rearrange("(p e) d -> p e d", e=PARITY)
             )
-            x_sb.append(x_b)
-        gb_rows = consts.tile([P, P], BF16)
-        nc.vector.memset(gb_rows[:], 0.0)
-        nc.sync.dma_start(
-            out=gb_rows[0:K_CHUNKS, :], in_=ln1_g.rearrange("(a p) -> a p", p=P)
-        )
-        nc.sync.dma_start(
-            out=gb_rows[K_CHUNKS : 2 * K_CHUNKS, :],
-            in_=ln1_b.rearrange("(a p) -> a p", p=P),
-        )
-        w_rows = W_qkv.rearrange("(a p) n -> p a n", p=P)
-        bias_bc = consts.tile([P, H, 3, HD], BF16)
-        wraw = []
+
+        w_rows = W_qkv.rearrange("(g t p) n -> g p t n", t=PACK, p=P)
+
+        def load_w(c, g):
+            nc.sync.dma_start(
+                out=wraw[c][g][:], in_=w_rows[g][:, :, CHUNK_COLS * c : CHUNK_COLS * (c + 1)]
+            )
+
+        load_x(0)
+        load_w(0, 0)
+        load_x(1)
+        load_w(0, 1)
         for c in range(CHUNKS):
-            w_c = wpool.tile([P, K_CHUNKS, CHUNK_COLS], BF16, name="wraw%d" % c)
             nc.sync.dma_start(
-                out=w_c[:], in_=w_rows[:, :, CHUNK_COLS * c : CHUNK_COLS * (c + 1)]
+                out=bias_bc[c][:].rearrange("p n d -> p (n d)"),
+                in_=b_qkv[CHUNK_COLS * c : CHUNK_COLS * (c + 1)].partition_broadcast(P),
             )
-            wraw.append(w_c)
-            if c == 0:
-                nc.sync.dma_start(
-                    out=bias_bc[:].rearrange("p h w d -> p (h w d)"),
-                    in_=b_qkv.partition_broadcast(P),
-                )
-
-        ident_f32 = consts.tile([P, P], F32)
-        make_identity(nc, ident_f32[:])
-        ident_bf16 = consts.tile([P, P], BF16)
-        nc.vector.tensor_copy(out=ident_bf16[:], in_=ident_f32[:])
-        neg_half = consts.tile([P, PARITY], F32)
-        nc.vector.memset(neg_half[:], -0.5)
+            if c + 1 < CHUNKS:
+                for g in range(PASSES):
+                    load_w(c + 1, g)
 
         pos_i = consts.tile([P, PARITY], I32)
         nc.gpsimd.iota(pos_i[:], pattern=[[1, PARITY]], base=0, channel_multiplier=PARITY)
+        ident_f32 = consts.tile([P, P], F32)
+        make_identity(nc, ident_f32[:])
+        neg_half = consts.tile([P, PARITY], F32)
+        nc.vector.memset(neg_half[:], -0.5)
+
         pos = consts.tile([P, PARITY], F32)
         nc.vector.tensor_copy(out=pos[:], in_=pos_i[:])
         turns = consts.tile([P, 2, PARITY, HALF], F32)
@@ -121,6 +147,8 @@ def tile_customgptneoxlayer_pa_kernel(
         )
         frac = consts.tile([P, 2, PARITY, HALF], F32)
         nc.vector.tensor_tensor(out=frac[:], in0=turns[:], in1=whole[:], op=ALU.subtract)
+        ident_bf16 = consts.tile([P, P], BF16)
+        nc.vector.tensor_copy(out=ident_bf16[:], in_=ident_f32[:])
         cos_tab = consts.tile([P, PARITY, 2, HALF], F32)
         sin_tab = consts.tile([P, PARITY, 2, HALF], F32)
         nc.scalar.activation(
@@ -135,25 +163,17 @@ def tile_customgptneoxlayer_pa_kernel(
         nc.scalar.activation(
             out=sin_tab[:, :, 1, :], in_=frac[:, 1], func=ACT.Sin, scale=2.0 * math.pi
         )
-
-        gb_t = psum.tile([P, P], BF16, tag="bank")
-        nc.tensor.transpose(gb_t[:], gb_rows[:], ident_bf16[:])
+        cos_qk = consts.tile([P, 2, PARITY, ROT], F32)
+        sin_qk = consts.tile([P, 2, PARITY, ROT], F32)
         gb_cols = consts.tile([P, 2 * K_CHUNKS], F32)
-        nc.vector.tensor_copy(out=gb_cols[:], in_=gb_t[:, 0 : 2 * K_CHUNKS])
 
-        xb = xpool.tile([P, K_CHUNKS, B * S], BF16)
-        xcodes = xpool.tile([P, PASSES, B * S], U32, align_bytes=64)
-        xscales = xpool.tile([P, PASSES, B * S], U8, align_bytes=64)
-        for b in range(B):
-            stats = xpool.tile(
-                [P, PARITY, D // BN_FMAX, BN_STATS_DIM], F32, name="stats%d" % b
-            )
+        def statistics(b):
+            stats = xpool.tile([P, PARITY, D // BN_FMAX, BN_STATS_DIM], F32, name="stats%d" % b)
             mean_var = xpool.tile([P, PARITY, 2], F32, name="mean_var%d" % b)
             for e in range(PARITY):
                 for f in range(D // BN_FMAX):
                     nc.vector.bn_stats(
-                        out=stats[:, e, f, :],
-                        in_=x_sb[b][:, e, BN_FMAX * f : BN_FMAX * (f + 1)],
+                        out=stats[:, e, f, :], in_=x_sb[b][:, e, BN_FMAX * f : BN_FMAX * (f + 1)]
                     )
                 nc.vector.bn_aggr(
                     out=mean_var[:, e, :], in_=stats[:, e].rearrange("p f s -> p (f s)")
@@ -168,171 +188,171 @@ def tile_customgptneoxlayer_pa_kernel(
             )
             rstd = xpool.tile([P, PARITY], F32, name="rstd%d" % b)
             nc.gpsimd.tensor_tensor(out=rstd[:], in0=var_eps[:], in1=neg_half[:], op=ALU.pow)
-            xn = xpool.tile([P, PARITY, D], F32, name="xn%d" % b)
             for e in range(PARITY):
                 nc.gpsimd.tensor_scalar(
-                    out=xn[:, e, :],
+                    out=xn[b][:, e, :],
                     in0=x_sb[b][:, e, :],
                     scalar1=neg_mean[:, e : e + 1],
                     scalar2=rstd[:, e : e + 1],
                     op0=ALU.add,
                     op1=ALU.mult,
                 )
-            cols = slice(S * b, S * (b + 1))
+
+        def transpose_x(b):
             for i in range(K_CHUNKS // 2):
-                xt = psum.tile([P, 2, S], F32, tag="bank")
+                xt = psum.tile([P, 2, S], F32, tag="bank", name="xt%d_%d" % (b, i))
                 for ai in range(2):
                     a = 2 * i + ai
                     for e in range(PARITY):
                         nc.tensor.transpose(
                             xt[:, ai, P * e : P * (e + 1)],
-                            xn[:, e, P * a : P * (a + 1)],
+                            xn[b][:, e, P * a : P * (a + 1)],
                             ident_f32[:],
                         )
                 for ai in range(2):
                     a = 2 * i + ai
-                    gain = gb_cols[:, a : a + 1]
-                    shift = gb_cols[:, K_CHUNKS + a : K_CHUNKS + a + 1]
-                    if i % 2 == 0:
-                        nc.scalar.activation(
-                            out=xb[:, a, cols],
-                            in_=xt[:, ai, :],
-                            func=ACT.Identity,
-                            scale=gain,
-                            bias=shift,
-                        )
-                    else:
-                        nc.vector.tensor_scalar(
-                            out=xb[:, a, cols],
-                            in0=xt[:, ai, :],
-                            scalar1=gain,
-                            scalar2=shift,
-                            op0=ALU.mult,
-                            op1=ALU.add,
-                        )
+                    nc.vector.tensor_scalar(
+                        out=xb[:, a, S * b : S * (b + 1)],
+                        in0=xt[:, ai, :],
+                        scalar1=gb_cols[:, a : a + 1],
+                        scalar2=gb_cols[:, K_CHUNKS + a : K_CHUNKS + a + 1],
+                        op0=ALU.mult,
+                        op1=ALU.add,
+                    )
+
+        def quantise_x(b):
+            cols = slice(S * b, S * (b + 1))
+            grouped = []
             for g in range(PASSES):
                 xg = xpool.tile([P, S, PACK], BF16, name="xg%d_%d" % (b, g), align_bytes=64)
                 regroup(nc.vector.tensor_copy, xg[:], xb[:, PACK * g : PACK * (g + 1), cols])
+                grouped.append(xg)
+            for g in range(PASSES):
                 nc.vector.quantize_mx(
                     out=xcodes[:, g, cols].bitcast(FP8X4),
                     scales=xscales[:, g, cols],
-                    in_=xg[:].rearrange("p c t -> p (c t)"),
+                    in_=grouped[g][:].rearrange("p c t -> p (c t)"),
                 )
 
-        wcodes = []
-        wscales = []
-
-        def prepare_weights(c):
-            codes = wpool.tile([P, PASSES, CHUNK_COLS], U32, name="wcodes%d" % c, align_bytes=64)
-            scales = wpool.tile([P, PASSES, CHUNK_COLS], U8, name="wscales%d" % c, align_bytes=64)
-            for g in range(PASSES):
-                rows = wraw[c][:, PACK * g : PACK * (g + 1), :]
-                wg_qk = stage.tile([P, QK_COLS, PACK], BF16, align_bytes=64)
-                wg_v = stage.tile([P, V_COLS, PACK], BF16, align_bytes=64)
-                for h in range(CHUNK_HEADS):
-                    head = HEAD_COLS * h
-                    regroup(
-                        nc.scalar.copy,
-                        wg_qk[:, 2 * HD * h : 2 * HD * (h + 1), :],
-                        rows[:, :, head : head + 2 * HD],
-                    )
-                    regroup(
-                        nc.vector.tensor_copy,
-                        wg_v[:, HD * h : HD * (h + 1), :],
-                        rows[:, :, head + 2 * HD : head + 3 * HD],
-                    )
+        def prepare_w(c, g):
+            wg = stage.tile([P, CHUNK_COLS, PACK], BF16, align_bytes=64, name="wg")
+            for part in (wide, narrow):
+                regroup(nc.scalar.copy, wg[:, part, :], wraw[c][g][:, :, part])
+            for part in (wide, narrow):
                 nc.vector.quantize_mx(
-                    out=codes[:, g, 0:QK_COLS].bitcast(FP8X4),
-                    scales=scales[:, g, 0:QK_COLS],
-                    in_=wg_qk[:].rearrange("p c t -> p (c t)"),
+                    out=wcodes[c][:, g, part].bitcast(FP8X4),
+                    scales=wscales[c][:, g, part],
+                    in_=wg[:, part, :].rearrange("p c t -> p (c t)"),
                 )
-                nc.vector.quantize_mx(
-                    out=codes[:, g, QK_COLS:CHUNK_COLS].bitcast(FP8X4),
-                    scales=scales[:, g, QK_COLS:CHUNK_COLS],
-                    in_=wg_v[:].rearrange("p c t -> p (c t)"),
-                )
-            wcodes.append(codes)
-            wscales.append(scales)
 
-        def mx_group(acc, b, e, c, w_cols):
+        def mx_group(acc, b, e, c, part):
             tokens = slice(S * b + P * e, S * b + P * (e + 1))
             for g in range(PASSES):
                 nc.tensor.matmul_mx(
                     out=acc,
                     lhsT=xcodes[:, g, tokens].bitcast(FP8X4),
                     lhsT_scale=xscales[:, g, tokens],
-                    rhs=wcodes[c][:, g, w_cols].bitcast(FP8X4),
-                    rhs_scale=wscales[c][:, g, w_cols],
+                    rhs=wcodes[c][:, g, part].bitcast(FP8X4),
+                    rhs_scale=wscales[c][:, g, part],
                     start=(g == 0),
                     stop=(g == PASSES - 1),
                 )
 
-        def project(c, b):
+        def store(c, b, w):
             heads = slice(CHUNK_HEADS * c, CHUNK_HEADS * (c + 1))
-            res = respool.tile([P, 3, CHUNK_HEADS, PARITY, HD], F32)
+            nc.sync.dma_start(
+                out=outs[w][b, heads].rearrange("h (p e) d -> p h (e d)", e=PARITY),
+                in_=res[c][:, b, :, w].rearrange("p h e d -> p h (e d)"),
+            )
+
+        def project(c, b):
+            blocks = res[c][:, b].rearrange("p h w e d -> p (h w) e d")
+            n_narrow = CHUNK_BLOCKS - WIDE_BLOCKS
+            acc_wide = []
             for e in range(PARITY):
-                acc_qk = psum.tile([P, CHUNK_HEADS, 2, HD], F32, tag="bank")
-                mx_group(acc_qk[:].rearrange("p h w d -> p (h w d)"), b, e, c, slice(0, QK_COLS))
+                acc = psum.tile([P, WIDE_BLOCKS, HD], F32, tag="bank", name="acc_wide%d" % e)
+                mx_group(acc[:].rearrange("p n d -> p (n d)"), b, e, c, wide)
+                acc_wide.append(acc)
+            acc_narrow = psum.tile([P, PARITY, n_narrow, HD], F32, tag="bank")
+            for e in range(PARITY):
+                mx_group(acc_narrow[:, e].rearrange("p n d -> p (n d)"), b, e, c, narrow)
+            for e in range(PARITY):
                 nc.vector.tensor_tensor(
-                    out=res[:, 0:2, :, e, :].rearrange("p w h d -> p h w d"),
-                    in0=acc_qk[:],
-                    in1=bias_bc[:, heads, 0:2, :],
+                    out=blocks[:, 0:WIDE_BLOCKS, e, :],
+                    in0=acc_wide[e][:],
+                    in1=bias_bc[c][:, 0:WIDE_BLOCKS, :],
                     op=ALU.add,
                 )
-            acc_v = psum.tile([P, PARITY, CHUNK_HEADS, HD], F32, tag="bank")
-            for e in range(PARITY):
-                mx_group(
-                    acc_v[:, e].rearrange("p h d -> p (h d)"), b, e, c, slice(QK_COLS, CHUNK_COLS)
-                )
             nc.vector.tensor_tensor(
-                out=res[:, 2].rearrange("p h e d -> p e h d"),
-                in0=acc_v[:],
-                in1=bias_bc[:, heads, 2, :].unsqueeze(1).to_broadcast([P, PARITY, CHUNK_HEADS, HD]),
+                out=blocks[:, WIDE_BLOCKS:CHUNK_BLOCKS].rearrange("p n e d -> p e n d"),
+                in0=acc_narrow[:],
+                in1=bias_bc[c][:, WIDE_BLOCKS:CHUNK_BLOCKS, :]
+                .unsqueeze(1)
+                .to_broadcast([P, PARITY, n_narrow, HD]),
                 op=ALU.add,
             )
-            nc.sync.dma_start(
-                out=outs[2][b, heads].rearrange("h (p e) d -> p h (e d)", e=PARITY),
-                in_=res[:, 2].rearrange("p h e d -> p h (e d)"),
+            store(c, b, 2)
+
+        def rotate(engine, c, first_b, n_b):
+            u = res[c][:, first_b : first_b + n_b, :, 0:2, :, 0:ROT].rearrange(
+                "p b h w e j -> p (b h) (w e) j"
             )
-            blocks = 2 * CHUNK_HEADS
-            u = res[:, 0:2, :, :, 0:ROT].rearrange("p w h e j -> p (w h) e j")
-            cos_b = (
-                cos_tab[:]
-                .rearrange("p e s j -> p e (s j)")
-                .unsqueeze(1)
-                .to_broadcast([P, blocks, PARITY, ROT])
-            )
-            sin_b = (
-                sin_tab[:]
-                .rearrange("p e s j -> p e (s j)")
-                .unsqueeze(1)
-                .to_broadcast([P, blocks, PARITY, ROT])
-            )
-            straight = respool.tile([P, blocks, PARITY, ROT], F32)
-            crossed = respool.tile([P, blocks, PARITY, ROT], F32)
-            nc.gpsimd.tensor_tensor(out=straight[:], in0=u, in1=cos_b, op=ALU.mult)
-            nc.gpsimd.tensor_tensor(
+            shape = [P, n_b * CHUNK_HEADS, 2 * PARITY, ROT]
+            cos_b = cos_qk[:].rearrange("p w e j -> p (w e) j").unsqueeze(1).to_broadcast(shape)
+            sin_b = sin_qk[:].rearrange("p w e j -> p (w e) j").unsqueeze(1).to_broadcast(shape)
+            straight = ropepool.tile(shape, F32, tag="straight")
+            crossed = ropepool.tile(shape, F32, tag="crossed")
+            engine.tensor_tensor(out=straight[:], in0=u, in1=cos_b, op=ALU.mult)
+            engine.tensor_tensor(
                 out=crossed[:, :, :, 0:HALF],
                 in0=u[:, :, :, HALF:ROT],
                 in1=sin_b[:, :, :, 0:HALF],
                 op=ALU.mult,
             )
-            nc.gpsimd.tensor_tensor(
+            engine.tensor_tensor(
                 out=crossed[:, :, :, HALF:ROT],
                 in0=u[:, :, :, 0:HALF],
                 in1=sin_b[:, :, :, HALF:ROT],
                 op=ALU.mult,
             )
-            nc.gpsimd.tensor_tensor(out=u, in0=straight[:], in1=crossed[:], op=ALU.add)
-            for w in range(2):
-                nc.sync.dma_start(
-                    out=outs[w][b, heads].rearrange("h (p e) d -> p h (e d)", e=PARITY),
-                    in_=res[:, w].rearrange("p h e d -> p h (e d)"),
-                )
+            engine.tensor_tensor(out=u, in0=straight[:], in1=crossed[:], op=ALU.add)
 
-        prepare_weights(0)
+        def store_qk(c, b):
+            store(c, b, 0)
+            store(c, b, 1)
+
+        param_t = psum.tile([P, P], BF16, tag="bank")
+        nc.tensor.transpose(param_t[:], param_rows[:], ident_bf16[:])
+        statistics(0)
+        nc.vector.tensor_copy(out=gb_cols[:], in_=param_t[:, 0 : 2 * K_CHUNKS])
+        for twice, tab in ((cos_qk, cos_tab), (sin_qk, sin_tab)):
+            nc.vector.tensor_copy(
+                out=twice[:],
+                in_=tab[:]
+                .rearrange("p e s j -> p e (s j)")
+                .unsqueeze(1)
+                .to_broadcast([P, 2, PARITY, ROT]),
+            )
+        statistics(1)
+        prepare_w(0, 0)
+        transpose_x(0)
+        quantise_x(0)
+        prepare_w(0, 1)
+        transpose_x(1)
+        quantise_x(1)
+
         for c in range(CHUNKS):
-            if c + 1 < CHUNKS:
-                prepare_weights(c + 1)
+            last = c == CHUNKS - 1
             for b in range(B):
+                if not last:
+                    prepare_w(c + 1, b)
                 project(c, b)
+                if b == 0 and c > 0:
+                    for earlier_b in range(B):
+                        store_qk(c - 1, earlier_b)
+                if last:
+                    rotate(nc.gpsimd if b == 0 else nc.vector, c, b, 1)
+            if not last:
+                rotate(nc.gpsimd, c, 0, B)
+        for b in range(B):
+            store_qk(CHUNKS - 1, b)

@@ -76,24 +76,18 @@ def tile_customgptneoxlayer_pa_kernel(
             wpool.tile([P, PASSES, CHUNK_COLS], U8, name="wscales%d" % c, align_bytes=64)
             for c in range(CHUNKS)
         ]
-        xb = xpool.tile([P, K_CHUNKS, B * S], BF16)
-        xcodes = xpool.tile([P, PASSES, B * S], U32, align_bytes=64)
-        xscales = xpool.tile([P, PASSES, B * S], U8, align_bytes=64)
+        xb = xpool.tile([P, B, K_CHUNKS, S], BF16)
+        xcodes = xpool.tile([P, B, PASSES, S], U32, align_bytes=64)
+        xscales = xpool.tile([P, B, PASSES, S], U8, align_bytes=64)
         res = [
             respool.tile([P, B, CHUNK_HEADS, 3, PARITY, HD], F32, name="res%d" % c)
             for c in range(CHUNKS)
         ]
 
-        nc.vector.memset(param_rows[:], 0.0)
-        nc.sync.dma_start(out=param_rows[0:K_CHUNKS, :], in_=ln1_g.rearrange("(a p) -> a p", p=P))
-        nc.sync.dma_start(
-            out=param_rows[K_CHUNKS : 2 * K_CHUNKS, :], in_=ln1_b.rearrange("(a p) -> a p", p=P)
-        )
-
         def load_x(b):
-            nc.sync.dma_start(
-                out=x_sb[b][:], in_=hidden_states[b].rearrange("(p e) d -> p e d", e=PARITY)
-            )
+            rows = hidden_states[b].rearrange("(p e) d -> p e d", e=PARITY)
+            for e in range(PARITY):
+                nc.sync.dma_start(out=x_sb[b][:, e, :], in_=rows[:, e, :])
 
         w_rows = W_qkv.rearrange("(g t p) n -> g p t n", t=PACK, p=P)
 
@@ -103,6 +97,11 @@ def tile_customgptneoxlayer_pa_kernel(
             )
 
         load_x(0)
+        nc.vector.memset(param_rows[:], 0.0)
+        nc.sync.dma_start(out=param_rows[0:K_CHUNKS, :], in_=ln1_g.rearrange("(a p) -> a p", p=P))
+        nc.sync.dma_start(
+            out=param_rows[K_CHUNKS : 2 * K_CHUNKS, :], in_=ln1_b.rearrange("(a p) -> a p", p=P)
+        )
         load_w(0, 0)
         load_x(1)
         load_w(0, 1)
@@ -179,12 +178,22 @@ def tile_customgptneoxlayer_pa_kernel(
                     out=mean_var[:, e, :], in_=stats[:, e].rearrange("p f s -> p (f s)")
                 )
             neg_mean = xpool.tile([P, PARITY], F32, name="neg_mean%d" % b)
-            nc.vector.tensor_scalar(
-                out=neg_mean[:], in0=mean_var[:, :, 0], scalar1=-1.0, scalar2=None, op0=ALU.mult
+            nc.gpsimd.tensor_scalar(
+                out=neg_mean[:],
+                in0=mean_var[:, :, 0],
+                scalar1=-1.0,
+                scalar2=0.0,
+                op0=ALU.mult,
+                op1=ALU.add,
             )
             var_eps = xpool.tile([P, PARITY], F32, name="var_eps%d" % b)
-            nc.vector.tensor_scalar(
-                out=var_eps[:], in0=mean_var[:, :, 1], scalar1=EPS, scalar2=None, op0=ALU.add
+            nc.gpsimd.tensor_scalar(
+                out=var_eps[:],
+                in0=mean_var[:, :, 1],
+                scalar1=1.0,
+                scalar2=EPS,
+                op0=ALU.mult,
+                op1=ALU.add,
             )
             rstd = xpool.tile([P, PARITY], F32, name="rstd%d" % b)
             nc.gpsimd.tensor_tensor(out=rstd[:], in0=var_eps[:], in1=neg_half[:], op=ALU.pow)
@@ -212,7 +221,7 @@ def tile_customgptneoxlayer_pa_kernel(
                 for ai in range(2):
                     a = 2 * i + ai
                     nc.vector.tensor_scalar(
-                        out=xb[:, a, S * b : S * (b + 1)],
+                        out=xb[:, b, a, :],
                         in0=xt[:, ai, :],
                         scalar1=gb_cols[:, a : a + 1],
                         scalar2=gb_cols[:, K_CHUNKS + a : K_CHUNKS + a + 1],
@@ -221,18 +230,14 @@ def tile_customgptneoxlayer_pa_kernel(
                     )
 
         def quantise_x(b):
-            cols = slice(S * b, S * (b + 1))
-            grouped = []
+            xg = xpool.tile([P, PASSES, S, PACK], BF16, name="xg%d" % b, align_bytes=64)
             for g in range(PASSES):
-                xg = xpool.tile([P, S, PACK], BF16, name="xg%d_%d" % (b, g), align_bytes=64)
-                regroup(nc.vector.tensor_copy, xg[:], xb[:, PACK * g : PACK * (g + 1), cols])
-                grouped.append(xg)
-            for g in range(PASSES):
-                nc.vector.quantize_mx(
-                    out=xcodes[:, g, cols].bitcast(FP8X4),
-                    scales=xscales[:, g, cols],
-                    in_=grouped[g][:].rearrange("p c t -> p (c t)"),
-                )
+                regroup(nc.vector.tensor_copy, xg[:, g], xb[:, b, PACK * g : PACK * (g + 1), :])
+            nc.vector.quantize_mx(
+                out=xcodes[:, b].rearrange("p g c -> p (g c)").bitcast(FP8X4),
+                scales=xscales[:, b].rearrange("p g c -> p (g c)"),
+                in_=xg[:].rearrange("p g c t -> p (g c t)"),
+            )
 
         def prepare_w(c, g):
             wg = stage.tile([P, CHUNK_COLS, PACK], BF16, align_bytes=64, name="wg")
@@ -246,12 +251,12 @@ def tile_customgptneoxlayer_pa_kernel(
                 )
 
         def mx_group(acc, b, e, c, part):
-            tokens = slice(S * b + P * e, S * b + P * (e + 1))
+            tokens = slice(P * e, P * (e + 1))
             for g in range(PASSES):
                 nc.tensor.matmul_mx(
                     out=acc,
-                    lhsT=xcodes[:, g, tokens].bitcast(FP8X4),
-                    lhsT_scale=xscales[:, g, tokens],
+                    lhsT=xcodes[:, b, g, tokens].bitcast(FP8X4),
+                    lhsT_scale=xscales[:, b, g, tokens],
                     rhs=wcodes[c][:, g, part].bitcast(FP8X4),
                     rhs_scale=wscales[c][:, g, part],
                     start=(g == 0),
@@ -293,11 +298,9 @@ def tile_customgptneoxlayer_pa_kernel(
             )
             store(c, b, 2)
 
-        def rotate(engine, c, first_b, n_b):
-            u = res[c][:, first_b : first_b + n_b, :, 0:2, :, 0:ROT].rearrange(
-                "p b h w e j -> p (b h) (w e) j"
-            )
-            shape = [P, n_b * CHUNK_HEADS, 2 * PARITY, ROT]
+        def rotate(engine, c, b):
+            u = res[c][:, b, :, 0:2, :, 0:ROT].rearrange("p h w e j -> p h (w e) j")
+            shape = [P, CHUNK_HEADS, 2 * PARITY, ROT]
             cos_b = cos_qk[:].rearrange("p w e j -> p (w e) j").unsqueeze(1).to_broadcast(shape)
             sin_b = sin_qk[:].rearrange("p w e j -> p (w e) j").unsqueeze(1).to_broadcast(shape)
             straight = ropepool.tile(shape, F32, tag="straight")
@@ -341,18 +344,12 @@ def tile_customgptneoxlayer_pa_kernel(
         transpose_x(1)
         quantise_x(1)
 
-        for c in range(CHUNKS):
-            last = c == CHUNKS - 1
-            for b in range(B):
-                if not last:
-                    prepare_w(c + 1, b)
-                project(c, b)
-                if b == 0 and c > 0:
-                    for earlier_b in range(B):
-                        store_qk(c - 1, earlier_b)
-                if last:
-                    rotate(nc.gpsimd if b == 0 else nc.vector, c, b, 1)
-            if not last:
-                rotate(nc.gpsimd, c, 0, B)
-        for b in range(B):
-            store_qk(CHUNKS - 1, b)
+        steps = [(c, b) for c in range(CHUNKS) for b in range(B)]
+        for i, (c, b) in enumerate(steps):
+            if c + 1 < CHUNKS:
+                prepare_w(c + 1, b)
+            project(c, b)
+            rotate(nc.gpsimd if i + 1 < len(steps) else nc.vector, c, b)
+            if i > 0:
+                store_qk(*steps[i - 1])
+        store_qk(*steps[-1])

@@ -178,22 +178,12 @@ def tile_customgptneoxlayer_pa_kernel(
                     out=mean_var[:, e, :], in_=stats[:, e].rearrange("p f s -> p (f s)")
                 )
             neg_mean = xpool.tile([P, PARITY], F32, name="neg_mean%d" % b)
-            nc.gpsimd.tensor_scalar(
-                out=neg_mean[:],
-                in0=mean_var[:, :, 0],
-                scalar1=-1.0,
-                scalar2=0.0,
-                op0=ALU.mult,
-                op1=ALU.add,
+            nc.vector.tensor_scalar(
+                out=neg_mean[:], in0=mean_var[:, :, 0], scalar1=-1.0, scalar2=None, op0=ALU.mult
             )
             var_eps = xpool.tile([P, PARITY], F32, name="var_eps%d" % b)
-            nc.gpsimd.tensor_scalar(
-                out=var_eps[:],
-                in0=mean_var[:, :, 1],
-                scalar1=1.0,
-                scalar2=EPS,
-                op0=ALU.mult,
-                op1=ALU.add,
+            nc.vector.tensor_scalar(
+                out=var_eps[:], in0=mean_var[:, :, 1], scalar1=EPS, scalar2=None, op0=ALU.add
             )
             rstd = xpool.tile([P, PARITY], F32, name="rstd%d" % b)
             nc.gpsimd.tensor_tensor(out=rstd[:], in0=var_eps[:], in1=neg_half[:], op=ALU.pow)
@@ -298,9 +288,11 @@ def tile_customgptneoxlayer_pa_kernel(
             )
             store(c, b, 2)
 
-        def rotate(engine, c, b):
-            u = res[c][:, b, :, 0:2, :, 0:ROT].rearrange("p h w e j -> p h (w e) j")
-            shape = [P, CHUNK_HEADS, 2 * PARITY, ROT]
+        def rotate(engine, c, first_b, n_b):
+            u = res[c][:, first_b : first_b + n_b, :, 0:2, :, 0:ROT].rearrange(
+                "p b h w e j -> p (b h) (w e) j"
+            )
+            shape = [P, n_b * CHUNK_HEADS, 2 * PARITY, ROT]
             cos_b = cos_qk[:].rearrange("p w e j -> p (w e) j").unsqueeze(1).to_broadcast(shape)
             sin_b = sin_qk[:].rearrange("p w e j -> p (w e) j").unsqueeze(1).to_broadcast(shape)
             straight = ropepool.tile(shape, F32, tag="straight")
@@ -344,12 +336,17 @@ def tile_customgptneoxlayer_pa_kernel(
         transpose_x(1)
         quantise_x(1)
 
-        steps = [(c, b) for c in range(CHUNKS) for b in range(B)]
-        for i, (c, b) in enumerate(steps):
-            if c + 1 < CHUNKS:
-                prepare_w(c + 1, b)
-            project(c, b)
-            rotate(nc.gpsimd if i + 1 < len(steps) else nc.vector, c, b)
-            if i > 0:
-                store_qk(*steps[i - 1])
-        store_qk(*steps[-1])
+        for c in range(CHUNKS):
+            last = c == CHUNKS - 1
+            for b in range(B):
+                if not last:
+                    prepare_w(c + 1, b)
+                project(c, b)
+                if last:
+                    rotate(nc.vector, c, b, 1)
+                    store_qk(c, b)
+                if b == 0 and c > 0:
+                    for earlier_b in range(B):
+                        store_qk(c - 1, earlier_b)
+            if not last:
+                rotate(nc.gpsimd, c, 0, B)

import math
from contextlib import ExitStack

import concourse.mybir as mybir
from concourse.masks import make_identity

F32 = mybir.dt.float32
BF16 = mybir.dt.bfloat16
I32 = mybir.dt.int32
U32 = mybir.dt.uint32
U8 = mybir.dt.uint8
FP8X4 = mybir.dt.float8_e4m3fn_x4
ALU = mybir.AluOpType
ACT = mybir.ActivationFunctionType

P = 128
B, S, D, H, HD = 2, 256, 1024, 8, 128
ROT = HD // 4
HALF = ROT // 2
EPS = 1e-5
ROPE_BASE = 10000.0
PACK = 4
PASSES = D // (P * PACK)
K_CHUNKS = D // P
PARITY = S // P
CHUNK_HEADS = 2
CHUNKS = H // CHUNK_HEADS
CHUNK_BLOCKS = 3 * CHUNK_HEADS
CHUNK_COLS = CHUNK_BLOCKS * HD
WIDE_BLOCKS = 4
WIDE_COLS = WIDE_BLOCKS * HD
BN_FMAX = 512
BN_STATS_DIM = 6
ROUND_MAGIC = 1.5 * 2.0**23

FLOPS = 2 * B * S * D * 3 * H * HD


def regroup(copy, dst, src):
    copy(
        out=dst.rearrange("p (c i) t -> p c t i", i=4),
        in_=src.rearrange("p t (c i) -> p c t i", i=4),
    )


def tile_customgptneoxlayer_pa_kernel(
    tc, hidden_states, ln1_g, ln1_b, W_qkv, b_qkv, out_0, out_1, out_2
):
    nc = tc.nc
    outs = (out_0, out_1, out_2)
    wide = slice(0, WIDE_COLS)
    narrow = slice(WIDE_COLS, CHUNK_COLS)
    with ExitStack() as stack:
        consts = stack.enter_context(tc.tile_pool(name="consts", bufs=1))
        xpool = stack.enter_context(tc.tile_pool(name="xpool", bufs=1))
        wpool = stack.enter_context(tc.tile_pool(name="wpool", bufs=1))
        stage = stack.enter_context(tc.tile_pool(name="stage", bufs=3))
        respool = stack.enter_context(tc.tile_pool(name="respool", bufs=1))
        ropepool = stack.enter_context(tc.tile_pool(name="ropepool", bufs=2))
        psum = stack.enter_context(tc.psum_pool(name="psum", bufs=8))
        stack.enter_context(tc.manual_schedule())

        param_rows = consts.tile([P, P], BF16)
        x_sb = [xpool.tile([P, PARITY, D], BF16, name="x_sb%d" % b) for b in range(B)]
        xn = [xpool.tile([P, PARITY, D], F32, name="xn%d" % b) for b in range(B)]
        wraw = [
            [wpool.tile([P, PACK, CHUNK_COLS], BF16, name="wraw%d_%d" % (c, g)) for g in range(PASSES)]
            for c in range(CHUNKS)
        ]
        bias_bc = [consts.tile([P, CHUNK_BLOCKS, HD], BF16, name="bias_bc%d" % c) for c in range(CHUNKS)]
        wcodes = [
            wpool.tile([P, PASSES, CHUNK_COLS], U32, name="wcodes%d" % c, align_bytes=64)
            for c in range(CHUNKS)
        ]
        wscales = [
            wpool.tile([P, PASSES, CHUNK_COLS], U8, name="wscales%d" % c, align_bytes=64)
            for c in range(CHUNKS)
        ]
        xb = xpool.tile([P, B, K_CHUNKS, S], BF16)
        xcodes = xpool.tile([P, B, PASSES, S], U32, align_bytes=64)
        xscales = xpool.tile([P, B, PASSES, S], U8, align_bytes=64)
        res = [
            respool.tile([P, B, CHUNK_HEADS, 3, PARITY, HD], F32, name="res%d" % c)
            for c in range(CHUNKS)
        ]

        def load_x(b):
            rows = hidden_states[b].rearrange("(p e) d -> p e d", e=PARITY)
            for e in range(PARITY):
                nc.sync.dma_start(out=x_sb[b][:, e, :], in_=rows[:, e, :])

        w_rows = W_qkv.rearrange("(g t p) n -> g p t n", t=PACK, p=P)

        def load_w(c, g):
            nc.sync.dma_start(
                out=wraw[c][g][:], in_=w_rows[g][:, :, CHUNK_COLS * c : CHUNK_COLS * (c + 1)]
            )

        load_x(0)
        nc.vector.memset(param_rows[:], 0.0)
        nc.sync.dma_start(out=param_rows[0:K_CHUNKS, :], in_=ln1_g.rearrange("(a p) -> a p", p=P))
        nc.sync.dma_start(
            out=param_rows[K_CHUNKS : 2 * K_CHUNKS, :], in_=ln1_b.rearrange("(a p) -> a p", p=P)
        )
        load_w(0, 0)
        load_x(1)
        load_w(0, 1)
        for c in range(CHUNKS):
            nc.sync.dma_start(
                out=bias_bc[c][:].rearrange("p n d -> p (n d)"),
                in_=b_qkv[CHUNK_COLS * c : CHUNK_COLS * (c + 1)].partition_broadcast(P),
            )
            if c + 1 < CHUNKS:
                for g in range(PASSES):
                    load_w(c + 1, g)

        pos_i = consts.tile([P, PARITY], I32)
        nc.gpsimd.iota(pos_i[:], pattern=[[1, PARITY]], base=0, channel_multiplier=PARITY)
        ident_f32 = consts.tile([P, P], F32)
        make_identity(nc, ident_f32[:])
        neg_half = consts.tile([P, PARITY], F32)
        nc.vector.memset(neg_half[:], -0.5)

        pos = consts.tile([P, PARITY], F32)
        nc.vector.tensor_copy(out=pos[:], in_=pos_i[:])
        turns = consts.tile([P, 2, PARITY, HALF], F32)
        for j in range(HALF):
            nc.vector.tensor_scalar(
                out=turns[:, 1, :, j],
                in0=pos[:],
                scalar1=ROPE_BASE ** (-j / HALF) / (2.0 * math.pi),
                scalar2=None,
                op0=ALU.mult,
            )
        nc.vector.tensor_scalar(
            out=turns[:, 0], in0=turns[:, 1], scalar1=0.25, scalar2=None, op0=ALU.add
        )
        whole = consts.tile([P, 2, PARITY, HALF], F32)
        nc.vector.tensor_scalar(
            out=whole[:],
            in0=turns[:],
            scalar1=ROUND_MAGIC,
            scalar2=ROUND_MAGIC,
            op0=ALU.add,
            op1=ALU.subtract,
        )
        frac = consts.tile([P, 2, PARITY, HALF], F32)
        nc.vector.tensor_tensor(out=frac[:], in0=turns[:], in1=whole[:], op=ALU.subtract)
        ident_bf16 = consts.tile([P, P], BF16)
        nc.vector.tensor_copy(out=ident_bf16[:], in_=ident_f32[:])
        cos_tab = consts.tile([P, PARITY, 2, HALF], F32)
        sin_tab = consts.tile([P, PARITY, 2, HALF], F32)
        nc.scalar.activation(
            out=cos_tab[:],
            in_=frac[:, 0].unsqueeze(2).to_broadcast([P, PARITY, 2, HALF]),
            func=ACT.Sin,
            scale=2.0 * math.pi,
        )
        nc.scalar.activation(
            out=sin_tab[:, :, 0, :], in_=frac[:, 1], func=ACT.Sin, scale=-2.0 * math.pi
        )
        nc.scalar.activation(
            out=sin_tab[:, :, 1, :], in_=frac[:, 1], func=ACT.Sin, scale=2.0 * math.pi
        )
        cos_qk = consts.tile([P, 2, PARITY, ROT], F32)
        sin_qk = consts.tile([P, 2, PARITY, ROT], F32)
        gb_cols = consts.tile([P, 2 * K_CHUNKS], F32)

        def statistics(b):
            stats = xpool.tile([P, PARITY, D // BN_FMAX, BN_STATS_DIM], F32, name="stats%d" % b)
            mean_var = xpool.tile([P, PARITY, 2], F32, name="mean_var%d" % b)
            for e in range(PARITY):
                for f in range(D // BN_FMAX):
                    nc.vector.bn_stats(
                        out=stats[:, e, f, :], in_=x_sb[b][:, e, BN_FMAX * f : BN_FMAX * (f + 1)]
                    )
                nc.vector.bn_aggr(
                    out=mean_var[:, e, :], in_=stats[:, e].rearrange("p f s -> p (f s)")
                )
            neg_mean = xpool.tile([P, PARITY], F32, name="neg_mean%d" % b)
            nc.vector.tensor_scalar(
                out=neg_mean[:], in0=mean_var[:, :, 0], scalar1=-1.0, scalar2=None, op0=ALU.mult
            )
            var_eps = xpool.tile([P, PARITY], F32, name="var_eps%d" % b)
            nc.vector.tensor_scalar(
                out=var_eps[:], in0=mean_var[:, :, 1], scalar1=EPS, scalar2=None, op0=ALU.add
            )
            rstd = xpool.tile([P, PARITY], F32, name="rstd%d" % b)
            nc.gpsimd.tensor_tensor(out=rstd[:], in0=var_eps[:], in1=neg_half[:], op=ALU.pow)
            for e in range(PARITY):
                nc.gpsimd.tensor_scalar(
                    out=xn[b][:, e, :],
                    in0=x_sb[b][:, e, :],
                    scalar1=neg_mean[:, e : e + 1],
                    scalar2=rstd[:, e : e + 1],
                    op0=ALU.add,
                    op1=ALU.mult,
                )

        def transpose_x(b):
            for i in range(K_CHUNKS // 2):
                xt = psum.tile([P, 2, S], F32, tag="bank", name="xt%d_%d" % (b, i))
                for ai in range(2):
                    a = 2 * i + ai
                    for e in range(PARITY):
                        nc.tensor.transpose(
                            xt[:, ai, P * e : P * (e + 1)],
                            xn[b][:, e, P * a : P * (a + 1)],
                            ident_f32[:],
                        )
                for ai in range(2):
                    a = 2 * i + ai
                    nc.vector.tensor_scalar(
                        out=xb[:, b, a, :],
                        in0=xt[:, ai, :],
                        scalar1=gb_cols[:, a : a + 1],
                        scalar2=gb_cols[:, K_CHUNKS + a : K_CHUNKS + a + 1],
                        op0=ALU.mult,
                        op1=ALU.add,
                    )

        def quantise_x(b):
            xg = xpool.tile([P, PASSES, S, PACK], BF16, name="xg%d" % b, align_bytes=64)
            for g in range(PASSES):
                regroup(nc.vector.tensor_copy, xg[:, g], xb[:, b, PACK * g : PACK * (g + 1), :])
            nc.vector.quantize_mx(
                out=xcodes[:, b].rearrange("p g c -> p (g c)").bitcast(FP8X4),
                scales=xscales[:, b].rearrange("p g c -> p (g c)"),
                in_=xg[:].rearrange("p g c t -> p (g c t)"),
            )

        def prepare_w(c, g):
            wg = stage.tile([P, CHUNK_COLS, PACK], BF16, align_bytes=64, name="wg")
            for part in (wide, narrow):
                regroup(nc.scalar.copy, wg[:, part, :], wraw[c][g][:, :, part])
            for part in (wide, narrow):
                nc.vector.quantize_mx(
                    out=wcodes[c][:, g, part].bitcast(FP8X4),
                    scales=wscales[c][:, g, part],
                    in_=wg[:, part, :].rearrange("p c t -> p (c t)"),
                )

        def mx_group(acc, b, e, c, part):
            tokens = slice(P * e, P * (e + 1))
            for g in range(PASSES):
                nc.tensor.matmul_mx(
                    out=acc,
                    lhsT=xcodes[:, b, g, tokens].bitcast(FP8X4),
                    lhsT_scale=xscales[:, b, g, tokens],
                    rhs=wcodes[c][:, g, part].bitcast(FP8X4),
                    rhs_scale=wscales[c][:, g, part],
                    start=(g == 0),
                    stop=(g == PASSES - 1),
                )

        def store(c, b, w):
            heads = slice(CHUNK_HEADS * c, CHUNK_HEADS * (c + 1))
            nc.sync.dma_start(
                out=outs[w][b, heads].rearrange("h (p e) d -> p h (e d)", e=PARITY),
                in_=res[c][:, b, :, w].rearrange("p h e d -> p h (e d)"),
            )

        def project(c, b):
            blocks = res[c][:, b].rearrange("p h w e d -> p (h w) e d")
            n_narrow = CHUNK_BLOCKS - WIDE_BLOCKS
            acc_wide = []
            for e in range(PARITY):
                acc = psum.tile([P, WIDE_BLOCKS, HD], F32, tag="bank", name="acc_wide%d" % e)
                mx_group(acc[:].rearrange("p n d -> p (n d)"), b, e, c, wide)
                acc_wide.append(acc)
            acc_narrow = psum.tile([P, PARITY, n_narrow, HD], F32, tag="bank")
            for e in range(PARITY):
                mx_group(acc_narrow[:, e].rearrange("p n d -> p (n d)"), b, e, c, narrow)
            for e in range(PARITY):
                nc.vector.tensor_tensor(
                    out=blocks[:, 0:WIDE_BLOCKS, e, :],
                    in0=acc_wide[e][:],
                    in1=bias_bc[c][:, 0:WIDE_BLOCKS, :],
                    op=ALU.add,
                )
            nc.vector.tensor_tensor(
                out=blocks[:, WIDE_BLOCKS:CHUNK_BLOCKS].rearrange("p n e d -> p e n d"),
                in0=acc_narrow[:],
                in1=bias_bc[c][:, WIDE_BLOCKS:CHUNK_BLOCKS, :]
                .unsqueeze(1)
                .to_broadcast([P, PARITY, n_narrow, HD]),
                op=ALU.add,
            )
            store(c, b, 2)

        def rotate(engine, c, first_b, n_b):
            u = res[c][:, first_b : first_b + n_b, :, 0:2, :, 0:ROT].rearrange(
                "p b h w e j -> p (b h) (w e) j"
            )
            shape = [P, n_b * CHUNK_HEADS, 2 * PARITY, ROT]
            cos_b = cos_qk[:].rearrange("p w e j -> p (w e) j").unsqueeze(1).to_broadcast(shape)
            sin_b = sin_qk[:].rearrange("p w e j -> p (w e) j").unsqueeze(1).to_broadcast(shape)
            straight = ropepool.tile(shape, F32, tag="straight")
            crossed = ropepool.tile(shape, F32, tag="crossed")
            engine.tensor_tensor(out=straight[:], in0=u, in1=cos_b, op=ALU.mult)
            engine.tensor_tensor(
                out=crossed[:, :, :, 0:HALF],
                in0=u[:, :, :, HALF:ROT],
                in1=sin_b[:, :, :, 0:HALF],
                op=ALU.mult,
            )
            engine.tensor_tensor(
                out=crossed[:, :, :, HALF:ROT],
                in0=u[:, :, :, 0:HALF],
                in1=sin_b[:, :, :, HALF:ROT],
                op=ALU.mult,
            )
            engine.tensor_tensor(out=u, in0=straight[:], in1=crossed[:], op=ALU.add)

        def store_qk(c, b):
            store(c, b, 0)
            store(c, b, 1)

        param_t = psum.tile([P, P], BF16, tag="bank")
        nc.tensor.transpose(param_t[:], param_rows[:], ident_bf16[:])
        statistics(0)
        nc.vector.tensor_copy(out=gb_cols[:], in_=param_t[:, 0 : 2 * K_CHUNKS])
        for twice, tab in ((cos_qk, cos_tab), (sin_qk, sin_tab)):
            nc.vector.tensor_copy(
                out=twice[:],
                in_=tab[:]
                .rearrange("p e s j -> p e (s j)")
                .unsqueeze(1)
                .to_broadcast([P, 2, PARITY, ROT]),
            )
        statistics(1)
        prepare_w(0, 0)
        transpose_x(0)
        quantise_x(0)
        prepare_w(0, 1)
        transpose_x(1)
        quantise_x(1)

        for c in range(CHUNKS):
            last = c == CHUNKS - 1
            for b in range(B):
                if not last:
                    prepare_w(c + 1, b)
                project(c, b)
                if last:
                    rotate(nc.vector, c, b, 1)
                    store_qk(c, b)
                if b == 0 and c > 0:
                    for earlier_b in range(B):
                        store_qk(c - 1, earlier_b)
            if not last:
                rotate(nc.gpsimd, c, 0, B)
